import numpy as np
import ml_dtypes


def mxq(x, axis, fmt="e4m3"):
    dtype, down = {"e4m3": (ml_dtypes.float8_e4m3fn, 7), "e5m2": (ml_dtypes.float8_e5m2, 14)}[fmt]
    v = np.moveaxis(np.asarray(x, np.float32).astype(ml_dtypes.bfloat16).astype(np.float64), axis, -1)
    blocks = v.reshape(v.shape[:-1] + (-1, 32))
    amax = np.abs(blocks).max(-1, keepdims=True)
    byte = np.maximum(np.where(amax > 0, np.frexp(amax)[1] - 1 + 127, 0) - down, 1)
    scale = np.exp2(byte - 127.0)
    codes = (blocks / scale).astype(np.float32).astype(dtype).astype(np.float64)
    return np.moveaxis((codes * scale).reshape(v.shape), -1, axis)


WIDE = False


def mx_kscale(k):
    if not WIDE:
        return np.ones(k)
    levels = np.array([10, -10, 5, -5, 0])
    a = np.random.permutation(np.resize(levels, k // 512 * 4)).reshape(k // 512, 4)
    idx = np.arange(k)
    return np.exp2(a[idx // 512, idx % 128 // 32])


BF16 = ml_dtypes.bfloat16


def bf(x):
    return np.asarray(x, np.float32).astype(BF16)


def f64(x):
    return np.asarray(x).astype(np.float64)


B, N, D, E, M, R = 1, 1024, 1024, 1024, 4096, 4
EPS = 1e-6


def layer_norm(v, g, b):
    mu = v.mean(-1, keepdims=True)
    var = ((v - mu) ** 2).mean(-1, keepdims=True)
    return (v - mu) / np.sqrt(var + EPS) * g + b


def merge(t):
    return t.reshape(B, N // R, R, E).mean(axis=2)


def setup_inputs():
    s = mx_kscale(D)

    def w():
        return bf(np.random.standard_normal((E, D)) * 2.0 / np.sqrt(D) / s)

    def c():
        return bf(np.random.standard_normal(E) * 0.3)

    x = np.random.standard_normal((B, N, D)) * (0.5 + 1.5 * np.random.random((B, N, 1))) + np.random.standard_normal((B, N, 1))
    return {"x": bf(x),
            "ln1_g": bf((1.0 + 0.1 * np.random.standard_normal(D)) * s),
            "ln1_b": bf(0.1 * np.random.standard_normal(D) * s),
            "Wq": w(), "bq": c(), "Wk": w(), "bk": c(), "Wv": w(), "bv": c()}


def reference(x, ln1_g, ln1_b, Wq, bq, Wk, bk, Wv, bv):
    h = layer_norm(f64(x), f64(ln1_g), f64(ln1_b))
    hq = mxq(h, 2, "e4m3")
    Q = (hq @ mxq(f64(Wq), 1, "e4m3").T) + f64(bq)
    K = (hq @ mxq(f64(Wk), 1, "e4m3").T) + f64(bk)
    V = (hq @ mxq(f64(Wv), 1, "e4m3").T) + f64(bv)
    return Q, merge(K), merge(V)

@@ -1,0 +1,317 @@
+from contextlib import ExitStack
+
+import concourse.mybir as mybir
+from concourse.masks import make_identity
+
+F32 = mybir.dt.float32
+BF16 = mybir.dt.bfloat16
+U32 = mybir.dt.uint32
+U8 = mybir.dt.uint8
+FP8X4 = mybir.dt.float8_e4m3fn_x4
+ACT = mybir.ActivationFunctionType
+ALU = mybir.AluOpType
+
+P = 128
+TOKENS = 1024
+D = 1024
+E = 1024
+MERGE = 4
+EPS = 1e-6
+PACK = 4
+K_PASS = P * PACK
+PASSES = D // K_PASS
+CHUNKS = D // P
+HALF = P * MERGE
+HALVES = TOKENS // HALF
+N_TILE = 512
+N_TILES = E // N_TILE
+RUN = N_TILE // P
+BN_MAX = 512
+
+FLOPS = 2 * 3 * TOKENS * D * E
+
+
+def tile_siglipencoderlayer_pa_kernel(
+    tc, x, ln1_g, ln1_b, Wq, bq, Wk, bk, Wv, bv, out_0, out_1, out_2
+):
+    nc = tc.nc
+    x_view = x.flatten_outer_dims().rearrange("(h j r) d -> j h r d", h=HALVES, r=MERGE)
+    q_view = out_0.flatten_outer_dims().rearrange("(h j r) e -> j h r e", h=HALVES, r=MERGE)
+    merged_views = {
+        "k": out_1.flatten_outer_dims().rearrange("(h j) e -> j h e", h=HALVES),
+        "v": out_2.flatten_outer_dims().rearrange("(h j) e -> j h e", h=HALVES),
+    }
+    weights = {"q": Wq, "k": Wk, "v": Wv}
+    biases = {"q": bq, "k": bk, "v": bv}
+
+    with ExitStack() as stack:
+        consts = stack.enter_context(tc.tile_pool(name="consts", bufs=1))
+        raw = stack.enter_context(tc.tile_pool(name="raw", bufs=1))
+        small = stack.enter_context(tc.tile_pool(name="small", bufs=2))
+        normed = stack.enter_context(tc.tile_pool(name="normed", bufs=2 * MERGE))
+        grouped = stack.enter_context(tc.tile_pool(name="grouped", bufs=3))
+        packed = stack.enter_context(tc.tile_pool(name="packed", bufs=1))
+        results = stack.enter_context(tc.tile_pool(name="results", bufs=6))
+        banks = stack.enter_context(tc.psum_pool(name="banks", bufs=8))
+        stack.enter_context(tc.manual_schedule())
+
+        ident = consts.tile([P, P], F32, name="ident")
+        make_identity(nc, ident[:])
+        eps = consts.tile([P, 1], F32, name="eps")
+        nc.vector.memset(eps[:], EPS)
+        warm = consts.tile([P, 1], F32, name="warm")
+        nc.scalar.activation(out=warm[:], in_=eps[:], func=ACT.Sqrt)
+
+        gb_rows = consts.tile([P, 2 * P], BF16, name="gb_rows")
+        nc.vector.memset(gb_rows[:], 0.0)
+        nc.scalar.dma_start(out=gb_rows[0:4, :], in_=ln1_g.rearrange("(c w) -> c w", c=4))
+        nc.scalar.dma_start(out=gb_rows[4:8, :], in_=ln1_b.rearrange("(c w) -> c w", c=4))
+
+        x_raw = [raw.tile([P, MERGE, D], BF16, name="x_raw%d" % h) for h in range(HALVES)]
+        w_raw = {n: raw.tile([P, N_TILES, RUN * D], BF16, name="w_raw_" + n) for n in "qkv"}
+        bias_all = {n: consts.tile([P, E], BF16, name="bias_all_" + n) for n in "qkv"}
+
+        def load_weight(n, nt, i):
+            rows = weights[n].rearrange("(nt i p) d -> p nt i d", nt=N_TILES, p=P)
+            nc.sync.dma_start(out=w_raw[n][:, nt, i * D : (i + 1) * D], in_=rows[:, nt, i, :])
+
+        def load_bias(n):
+            nc.sync.dma_start(out=bias_all[n][:], in_=biases[n].partition_broadcast(P))
+
+        for i in range(RUN):
+            nc.sync.dma_start(out=x_raw[0][:, i, :], in_=x_view[:, 0, i, :])
+            load_weight("q", 0, i)
+        nc.sync.dma_start(out=x_raw[1][:], in_=x_view[:, 1, :, :])
+        for i in range(RUN):
+            load_weight("q", 1, i)
+        load_bias("q")
+        for n in "kv":
+            for nt in range(N_TILES):
+                for i in range(RUN):
+                    load_weight(n, nt, i)
+            load_bias(n)
+
+        gain_bias = consts.tile([P, 2 * CHUNKS], F32, name="gain_bias")
+        h_planes = packed.tile([P, CHUNKS, TOKENS], BF16, name="h_planes")
+        h_words = packed.tile([P, PASSES, TOKENS], U32, name="h_words", align_bytes=64)
+        h_scales = packed.tile([P, PASSES, TOKENS], U8, name="h_scales", align_bytes=64)
+        w_words = {
+            n: packed.tile([P, N_TILES, PASSES * N_TILE], U32, name="w_words_" + n, align_bytes=64)
+            for n in "qkv"
+        }
+        w_scales = {
+            n: packed.tile([P, N_TILES, PASSES * N_TILE], U8, name="w_scales_" + n, align_bytes=64)
+            for n in "qkv"
+        }
+        w_grouped = {}
+        xn_tiles = {}
+        moments = {}
+        mean_vars = {}
+
+        def flip_gain_bias():
+            bank = banks.tile([P, N_TILE], F32, tag="bank")
+            nc.tensor.transpose(out=bank[:, 0:P], in_=gb_rows[:].bitcast(F32), identity=ident[:])
+            nc.vector.tensor_copy(out=gain_bias[:], in_=bank[:].bitcast(BF16)[:, 0 : 2 * CHUNKS])
+
+        def flip_weight_bank(n, nt, i, engine):
+            if i == 0:
+                w_grouped[(n, nt)] = grouped.tile(
+                    [P, PASSES * N_TILE * PACK], BF16, name="w_grouped", tag="w_grouped", align_bytes=64
+                )
+            words_in = w_raw[n][:, nt, :].bitcast(F32).rearrange(
+                "p (i c q) -> p i c q", i=RUN, c=PASSES * 2
+            )
+            words_out = w_grouped[(n, nt)][:].bitcast(F32).rearrange(
+                "p (g e u) -> p g e u", g=PASSES, u=2
+            )
+            bank = banks.tile([P, N_TILE], F32, tag="bank")
+            for c in range(PASSES * 2):
+                nc.tensor.transpose(
+                    out=bank[:, c * P : (c + 1) * P], in_=words_in[:, i, c, :], identity=ident[:]
+                )
+            dst = words_out[:, :, i * P : (i + 1) * P, :]
+            src = bank[:].rearrange("p (g u e) -> p g e u", g=PASSES, u=2)
+            if engine == "vector":
+                nc.vector.tensor_copy(out=dst, in_=src)
+            else:
+                nc.scalar.copy(out=dst, in_=src)
+
+        def flip_weight(n, nt, vector_banks):
+            for i in range(RUN):
+                flip_weight_bank(n, nt, i, "vector" if i < vector_banks else "scalar")
+
+        def pack_weight(n, nt):
+            nc.vector.quantize_mx(
+                out=w_words[n][:, nt, :].bitcast(FP8X4),
+                scales=w_scales[n][:, nt, :],
+                in_=w_grouped[(n, nt)][:],
+            )
+
+        def measure_tile(h, r):
+            if r == 0:
+                mean_vars[h] = small.tile([P, MERGE, 2], F32, name="mean_var", tag="mean_var")
+            stats = small.tile([P, D // BN_MAX, 6], F32, tag="stats")
+            for s in range(D // BN_MAX):
+                nc.vector.bn_stats(
+                    out=stats[:, s, :], in_=x_raw[h][:, r, s * BN_MAX : (s + 1) * BN_MAX]
+                )
+            nc.vector.bn_aggr(out=mean_vars[h][:, r, :], in_=stats[:].rearrange("p s k -> p (s k)"))
+
+        def finish_measure(h):
+            mean_var = mean_vars[h]
+            std = small.tile([P, MERGE], F32, tag="std")
+            nc.scalar.activation(out=std[:], in_=mean_var[:, :, 1], func=ACT.Sqrt, bias=eps[:, 0:1])
+            rstd = small.tile([P, MERGE], F32, tag="rstd")
+            nc.vector.reciprocal(out=rstd[:], in_=std[:])
+            shift = small.tile([P, MERGE], F32, tag="shift")
+            nc.vector.scalar_tensor_tensor(
+                out=shift[:], in0=mean_var[:, :, 0], scalar=-1.0, in1=rstd[:], op0=ALU.mult, op1=ALU.mult
+            )
+            moments[h] = (rstd, shift)
+
+        def normalise(h, r, engine):
+            rstd, shift = moments[h]
+            xn = normed.tile([P, D], F32, tag="xn")
+            xn_tiles[(h, r)] = xn
+            dst = xn[:].rearrange("p (c e q) -> p c e q", c=PASSES * 2, e=2)
+            src = x_raw[h][:, r, :].rearrange("p (c q e) -> p c e q", c=PASSES * 2, e=2)
+            if engine == "scalar":
+                nc.scalar.activation(
+                    out=dst, in_=src, func=ACT.Identity, scale=rstd[:, r : r + 1], bias=shift[:, r : r + 1]
+                )
+            elif engine == "vector":
+                nc.vector.tensor_scalar(
+                    out=dst, in0=src, scalar1=rstd[:, r : r + 1], scalar2=shift[:, r : r + 1],
+                    op0=ALU.mult, op1=ALU.add,
+                )
+            else:
+                nc.gpsimd.tensor_scalar(
+                    out=dst, in0=src, scalar1=rstd[:, r : r + 1], scalar2=shift[:, r : r + 1],
+                    op0=ALU.mult, op1=ALU.add,
+                )
+
+        def flip_tokens(h, g, vector_banks):
+            toks = slice(h * HALF, (h + 1) * HALF)
+            for t in range(PACK):
+                f = g * PACK + t
+                bank = banks.tile([P, N_TILE], F32, tag="bank")
+                for r in range(MERGE):
+                    nc.tensor.transpose(
+                        out=bank[:, r * P : (r + 1) * P],
+                        in_=xn_tiles[(h, r)][:, f * P : (f + 1) * P],
+                        identity=ident[:],
+                    )
+                gain = gain_bias[:, f : f + 1]
+                bias = gain_bias[:, CHUNKS + f : CHUNKS + f + 1]
+                if t < vector_banks:
+                    nc.vector.tensor_scalar(
+                        out=h_planes[:, f, toks], in0=bank[:], scalar1=gain, scalar2=bias,
+                        op0=ALU.mult, op1=ALU.add,
+                    )
+                else:
+                    nc.scalar.activation(
+                        out=h_planes[:, f, toks], in_=bank[:], func=ACT.Identity, scale=gain, bias=bias
+                    )
+
+        h_grouped = {}
+
+        def group_tokens(h, g, engine):
+            toks = slice(h * HALF, (h + 1) * HALF)
+            tile_ = grouped.tile([P, HALF * PACK], BF16, tag="h_grouped", align_bytes=64)
+            h_grouped[(h, g)] = tile_
+            dst = tile_[:].rearrange("p (n t) -> p n t", t=PACK)
+            src = h_planes[:, g * PACK : (g + 1) * PACK, toks].rearrange("p t n -> p n t")
+            if engine == "vector":
+                nc.vector.tensor_copy(out=dst, in_=src)
+            else:
+                nc.scalar.copy(out=dst, in_=src)
+
+        def pack_tokens(h, g):
+            toks = slice(h * HALF, (h + 1) * HALF)
+            nc.vector.quantize_mx(
+                out=h_words[:, g, toks].bitcast(FP8X4), scales=h_scales[:, g, toks],
+                in_=h_grouped[(h, g)][:],
+            )
+
+        def one_pass(acc, n, h, r, g, nt, start, stop):
+            toks = slice(h * HALF + r * P, h * HALF + (r + 1) * P)
+            cols = slice(g * N_TILE, (g + 1) * N_TILE)
+            nc.tensor.matmul_mx(
+                out=acc[:],
+                lhsT=h_words[:, g, toks].bitcast(FP8X4),
+                lhsT_scale=h_scales[:, g, toks],
+                rhs=w_words[n][:, nt, cols].bitcast(FP8X4),
+                rhs_scale=w_scales[n][:, nt, cols],
+                start=start,
+                stop=stop,
+            )
+
+        def queries(h, nt):
+            cols = slice(nt * N_TILE, (nt + 1) * N_TILE)
+            for r in range(MERGE):
+                acc = banks.tile([P, N_TILE], F32, tag="bank")
+                for g in range(PASSES):
+                    one_pass(acc, "q", h, r, g, nt, g == 0, g == PASSES - 1)
+                rows = results.tile([P, N_TILE], F32, tag="rows")
+                nc.vector.tensor_tensor(out=rows[:], in0=acc[:], in1=bias_all["q"][:, cols], op=ALU.add)
+                nc.sync.dma_start(out=q_view[:, h, r, cols], in_=rows[:])
+
+        def merged(n, h, nt):
+            cols = slice(nt * N_TILE, (nt + 1) * N_TILE)
+            acc = banks.tile([P, N_TILE], F32, tag="bank")
+            for r in range(MERGE):
+                for g in range(PASSES):
+                    one_pass(acc, n, h, r, g, nt, r == 0 and g == 0, r == MERGE - 1 and g == PASSES - 1)
+            rows = results.tile([P, N_TILE], F32, tag="rows")
+            nc.vector.scalar_tensor_tensor(
+                out=rows[:], in0=acc[:], scalar=1.0 / MERGE, in1=bias_all[n][:, cols],
+                op0=ALU.mult, op1=ALU.add,
+            )
+            nc.sync.dma_start(out=merged_views[n][:, h, cols], in_=rows[:])
+
+        for i in range(RUN):
+            measure_tile(0, i)
+            flip_weight_bank("q", 0, i, "scalar")
+        finish_measure(0)
+        flip_gain_bias()
+        for r in range(MERGE):
+            normalise(0, r, "gpsimd" if r % 2 == 0 else "scalar")
+        for r in range(MERGE):
+            measure_tile(1, r)
+        flip_tokens(0, 0, 0)
+        flip_tokens(0, 1, 0)
+        pack_weight("q", 0)
+        group_tokens(0, 0, "vector")
+        pack_tokens(0, 0)
+        group_tokens(0, 1, "vector")
+        pack_tokens(0, 1)
+        finish_measure(1)
+        flip_weight("q", 1, 0)
+        for r in range(MERGE):
+            normalise(1, r, "gpsimd" if r % 2 == 0 else "scalar")
+        queries(0, 0)
+        pack_weight("q", 1)
+        flip_tokens(1, 0, 0)
+        flip_tokens(1, 1, 0)
+        queries(0, 1)
+        group_tokens(1, 0, "vector")
+        pack_tokens(1, 0)
+        flip_weight("k", 0, 0)
+        group_tokens(1, 1, "vector")
+        pack_tokens(1, 1)
+        flip_weight("k", 1, 0)
+        queries(1, 0)
+        pack_weight("k", 0)
+        queries(1, 1)
+        pack_weight("k", 1)
+        flip_weight("v", 0, 0)
+        merged("k", 0, 0)
+        merged("k", 1, 0)
+        flip_weight("v", 1, 0)
+        pack_weight("v", 0)
+        merged("k", 0, 1)
+        merged("k", 1, 1)
+        pack_weight("v", 1)
+        for nt in range(N_TILES):
+            for h in range(HALVES):
+                merged("v", h, nt)

@@ -48,10 +48,10 @@ def tile_siglipencoderlayer_pa_kernel(
         consts = stack.enter_context(tc.tile_pool(name="consts", bufs=1))
         raw = stack.enter_context(tc.tile_pool(name="raw", bufs=1))
         small = stack.enter_context(tc.tile_pool(name="small", bufs=2))
-        normed = stack.enter_context(tc.tile_pool(name="normed", bufs=2 * MERGE))
+        normed = stack.enter_context(tc.tile_pool(name="normed", bufs=MERGE + 2))
         grouped = stack.enter_context(tc.tile_pool(name="grouped", bufs=3))
         packed = stack.enter_context(tc.tile_pool(name="packed", bufs=1))
-        results = stack.enter_context(tc.tile_pool(name="results", bufs=6))
+        results = stack.enter_context(tc.tile_pool(name="results", bufs=16))
         banks = stack.enter_context(tc.psum_pool(name="banks", bufs=8))
         stack.enter_context(tc.manual_schedule())
 
@@ -89,6 +89,7 @@ def tile_siglipencoderlayer_pa_kernel(
             for nt in range(N_TILES):
                 for i in range(RUN):
                     load_weight(n, nt, i)
+        for n in "kv":
             load_bias(n)
 
         gain_bias = consts.tile([P, 2 * CHUNKS], F32, name="gain_bias")

@@ -27,6 +27,10 @@ N_TILE = 512
 N_TILES = E // N_TILE
 RUN = N_TILE // P
 BN_MAX = 512
+TILES = TOKENS // P
+UNIT_TILES = 2
+UNITS = TILES // UNIT_TILES
+UNIT = UNIT_TILES * P
 
 FLOPS = 2 * 3 * TOKENS * D * E
 
@@ -48,54 +52,56 @@ def tile_siglipencoderlayer_pa_kernel(
         consts = stack.enter_context(tc.tile_pool(name="consts", bufs=1))
         raw = stack.enter_context(tc.tile_pool(name="raw", bufs=1))
         small = stack.enter_context(tc.tile_pool(name="small", bufs=2))
-        normed = stack.enter_context(tc.tile_pool(name="normed", bufs=MERGE + 2))
+        normed = stack.enter_context(tc.tile_pool(name="normed", bufs=6))
         grouped = stack.enter_context(tc.tile_pool(name="grouped", bufs=3))
         packed = stack.enter_context(tc.tile_pool(name="packed", bufs=1))
-        results = stack.enter_context(tc.tile_pool(name="results", bufs=16))
+        results = stack.enter_context(tc.tile_pool(name="results", bufs=8))
         banks = stack.enter_context(tc.psum_pool(name="banks", bufs=8))
         stack.enter_context(tc.manual_schedule())
 
         ident = consts.tile([P, P], F32, name="ident")
         make_identity(nc, ident[:])
-        eps = consts.tile([P, 1], F32, name="eps")
-        nc.vector.memset(eps[:], EPS)
-        warm = consts.tile([P, 1], F32, name="warm")
-        nc.scalar.activation(out=warm[:], in_=eps[:], func=ACT.Sqrt)
 
         gb_rows = consts.tile([P, 2 * P], BF16, name="gb_rows")
         nc.vector.memset(gb_rows[:], 0.0)
         nc.scalar.dma_start(out=gb_rows[0:4, :], in_=ln1_g.rearrange("(c w) -> c w", c=4))
         nc.scalar.dma_start(out=gb_rows[4:8, :], in_=ln1_b.rearrange("(c w) -> c w", c=4))
 
-        x_raw = [raw.tile([P, MERGE, D], BF16, name="x_raw%d" % h) for h in range(HALVES)]
+        x_raw = [raw.tile([P, D], BF16, name="x_raw%d" % i) for i in range(TILES)]
         w_raw = {n: raw.tile([P, N_TILES, RUN * D], BF16, name="w_raw_" + n) for n in "qkv"}
+        bias_rows = consts.tile([P, 3 * E], BF16, name="bias_rows")
+        nc.vector.memset(bias_rows[:], 0.0)
+        for k, n in enumerate("qkv"):
+            nc.scalar.dma_start(
+                out=bias_rows[0:1, k * E : (k + 1) * E], in_=biases[n].rearrange("(o e) -> o e", o=1)
+            )
+        ones = consts.tile([P, P], BF16, name="ones")
+        nc.vector.memset(ones[:], 1.0)
         bias_all = {n: consts.tile([P, E], BF16, name="bias_all_" + n) for n in "qkv"}
+        eps = consts.tile([P, 1], F32, name="eps")
+        nc.vector.memset(eps[:], EPS)
+        warm = consts.tile([P, 1], F32, name="warm")
+        nc.scalar.activation(out=warm[:], in_=eps[:], func=ACT.Sqrt)
+
+        def load_tokens(i):
+            nc.sync.dma_start(out=x_raw[i][:], in_=x_view[:, i // MERGE, i % MERGE, :])
 
         def load_weight(n, nt, i):
             rows = weights[n].rearrange("(nt i p) d -> p nt i d", nt=N_TILES, p=P)
             nc.sync.dma_start(out=w_raw[n][:, nt, i * D : (i + 1) * D], in_=rows[:, nt, i, :])
 
-        def load_bias(n):
-            nc.sync.dma_start(out=bias_all[n][:], in_=biases[n].partition_broadcast(P))
-
-        for i in range(RUN):
-            nc.sync.dma_start(out=x_raw[0][:, i, :], in_=x_view[:, 0, i, :])
-            load_weight("q", 0, i)
-        nc.sync.dma_start(out=x_raw[1][:], in_=x_view[:, 1, :, :])
-        for i in range(RUN):
-            load_weight("q", 1, i)
-        load_bias("q")
+        for i in range(TILES):
+            load_tokens(i)
+            load_weight("q", i // RUN, i % RUN)
         for n in "kv":
             for nt in range(N_TILES):
                 for i in range(RUN):
                     load_weight(n, nt, i)
-        for n in "kv":
-            load_bias(n)
 
         gain_bias = consts.tile([P, 2 * CHUNKS], F32, name="gain_bias")
         h_planes = packed.tile([P, CHUNKS, TOKENS], BF16, name="h_planes")
-        h_words = packed.tile([P, PASSES, TOKENS], U32, name="h_words", align_bytes=64)
-        h_scales = packed.tile([P, PASSES, TOKENS], U8, name="h_scales", align_bytes=64)
+        h_words = packed.tile([P, UNITS, PASSES * UNIT], U32, name="h_words", align_bytes=64)
+        h_scales = packed.tile([P, UNITS, PASSES * UNIT], U8, name="h_scales", align_bytes=64)
         w_words = {
             n: packed.tile([P, N_TILES, PASSES * N_TILE], U32, name="w_words_" + n, align_bytes=64)
             for n in "qkv"
@@ -107,7 +113,20 @@ def tile_siglipencoderlayer_pa_kernel(
         w_grouped = {}
         xn_tiles = {}
         moments = {}
-        mean_vars = {}
+
+        def spread_bias(n):
+            first = "qkv".index(n) * E
+            bank = banks.tile([P, E], BF16, tag="bank")
+            for nt in range(N_TILES):
+                cols = slice(nt * N_TILE, (nt + 1) * N_TILE)
+                nc.tensor.matmul(
+                    out=bank[:, cols],
+                    lhsT=ones[:],
+                    rhs=bias_rows[:, first + nt * N_TILE : first + (nt + 1) * N_TILE],
+                    start=True,
+                    stop=True,
+                )
+            nc.scalar.copy(out=bias_all[n][:], in_=bank[:])
 
         def flip_gain_bias():
             bank = banks.tile([P, N_TILE], F32, tag="bank")
@@ -148,121 +167,125 @@ def tile_siglipencoderlayer_pa_kernel(
                 in_=w_grouped[(n, nt)][:],
             )
 
-        def measure_tile(h, r):
-            if r == 0:
-                mean_vars[h] = small.tile([P, MERGE, 2], F32, name="mean_var", tag="mean_var")
-            stats = small.tile([P, D // BN_MAX, 6], F32, tag="stats")
-            for s in range(D // BN_MAX):
-                nc.vector.bn_stats(
-                    out=stats[:, s, :], in_=x_raw[h][:, r, s * BN_MAX : (s + 1) * BN_MAX]
-                )
-            nc.vector.bn_aggr(out=mean_vars[h][:, r, :], in_=stats[:].rearrange("p s k -> p (s k)"))
-
-        def finish_measure(h):
-            mean_var = mean_vars[h]
-            std = small.tile([P, MERGE], F32, tag="std")
+        def measure(u):
+            mean_var = small.tile([P, UNIT_TILES, 2], F32, tag="mean_var")
+            for a in range(UNIT_TILES):
+                stats = small.tile([P, D // BN_MAX, 6], F32, tag="stats")
+                for s in range(D // BN_MAX):
+                    nc.vector.bn_stats(
+                        out=stats[:, s, :], in_=x_raw[u * UNIT_TILES + a][:, s * BN_MAX : (s + 1) * BN_MAX]
+                    )
+                nc.vector.bn_aggr(out=mean_var[:, a, :], in_=stats[:].rearrange("p s k -> p (s k)"))
+            std = small.tile([P, UNIT_TILES], F32, tag="std")
             nc.scalar.activation(out=std[:], in_=mean_var[:, :, 1], func=ACT.Sqrt, bias=eps[:, 0:1])
-            rstd = small.tile([P, MERGE], F32, tag="rstd")
+            rstd = small.tile([P, UNIT_TILES], F32, tag="rstd")
             nc.vector.reciprocal(out=rstd[:], in_=std[:])
-            shift = small.tile([P, MERGE], F32, tag="shift")
+            shift = small.tile([P, UNIT_TILES], F32, tag="shift")
             nc.vector.scalar_tensor_tensor(
                 out=shift[:], in0=mean_var[:, :, 0], scalar=-1.0, in1=rstd[:], op0=ALU.mult, op1=ALU.mult
             )
-            moments[h] = (rstd, shift)
+            moments[u] = (rstd, shift)
 
-        def normalise(h, r, engine):
-            rstd, shift = moments[h]
+        def normalise(u, a, engine):
+            rstd, shift = moments[u]
             xn = normed.tile([P, D], F32, tag="xn")
-            xn_tiles[(h, r)] = xn
+            xn_tiles[(u, a)] = xn
             dst = xn[:].rearrange("p (c e q) -> p c e q", c=PASSES * 2, e=2)
-            src = x_raw[h][:, r, :].rearrange("p (c q e) -> p c e q", c=PASSES * 2, e=2)
+            src = x_raw[u * UNIT_TILES + a][:].rearrange("p (c q e) -> p c e q", c=PASSES * 2, e=2)
             if engine == "scalar":
                 nc.scalar.activation(
-                    out=dst, in_=src, func=ACT.Identity, scale=rstd[:, r : r + 1], bias=shift[:, r : r + 1]
-                )
-            elif engine == "vector":
-                nc.vector.tensor_scalar(
-                    out=dst, in0=src, scalar1=rstd[:, r : r + 1], scalar2=shift[:, r : r + 1],
-                    op0=ALU.mult, op1=ALU.add,
+                    out=dst, in_=src, func=ACT.Identity, scale=rstd[:, a : a + 1], bias=shift[:, a : a + 1]
                 )
             else:
                 nc.gpsimd.tensor_scalar(
-                    out=dst, in0=src, scalar1=rstd[:, r : r + 1], scalar2=shift[:, r : r + 1],
+                    out=dst, in0=src, scalar1=rstd[:, a : a + 1], scalar2=shift[:, a : a + 1],
                     op0=ALU.mult, op1=ALU.add,
                 )
 
-        def flip_tokens(h, g, vector_banks):
-            toks = slice(h * HALF, (h + 1) * HALF)
-            for t in range(PACK):
-                f = g * PACK + t
+        def flip_tokens(u, vector_banks):
+            toks = slice(u * UNIT, (u + 1) * UNIT)
+            per_bank = RUN // UNIT_TILES
+            for b in range(CHUNKS // per_bank):
                 bank = banks.tile([P, N_TILE], F32, tag="bank")
-                for r in range(MERGE):
-                    nc.tensor.transpose(
-                        out=bank[:, r * P : (r + 1) * P],
-                        in_=xn_tiles[(h, r)][:, f * P : (f + 1) * P],
-                        identity=ident[:],
-                    )
-                gain = gain_bias[:, f : f + 1]
-                bias = gain_bias[:, CHUNKS + f : CHUNKS + f + 1]
-                if t < vector_banks:
-                    nc.vector.tensor_scalar(
-                        out=h_planes[:, f, toks], in0=bank[:], scalar1=gain, scalar2=bias,
-                        op0=ALU.mult, op1=ALU.add,
-                    )
-                else:
-                    nc.scalar.activation(
-                        out=h_planes[:, f, toks], in_=bank[:], func=ACT.Identity, scale=gain, bias=bias
-                    )
+                for k in range(per_bank):
+                    f = b * per_bank + k
+                    for a in range(UNIT_TILES):
+                        col = (k * UNIT_TILES + a) * P
+                        nc.tensor.transpose(
+                            out=bank[:, col : col + P],
+                            in_=xn_tiles[(u, a)][:, f * P : (f + 1) * P],
+                            identity=ident[:],
+                        )
+                for k in range(per_bank):
+                    f = b * per_bank + k
+                    gain = gain_bias[:, f : f + 1]
+                    bias = gain_bias[:, CHUNKS + f : CHUNKS + f + 1]
+                    src = bank[:, k * UNIT : (k + 1) * UNIT]
+                    if b < vector_banks:
+                        nc.vector.tensor_scalar(
+                            out=h_planes[:, f, toks], in0=src, scalar1=gain, scalar2=bias,
+                            op0=ALU.mult, op1=ALU.add,
+                        )
+                    else:
+                        nc.scalar.activation(
+                            out=h_planes[:, f, toks], in_=src, func=ACT.Identity, scale=gain, bias=bias
+                        )
 
         h_grouped = {}
 
-        def group_tokens(h, g, engine):
-            toks = slice(h * HALF, (h + 1) * HALF)
-            tile_ = grouped.tile([P, HALF * PACK], BF16, tag="h_grouped", align_bytes=64)
-            h_grouped[(h, g)] = tile_
-            dst = tile_[:].rearrange("p (n t) -> p n t", t=PACK)
-            src = h_planes[:, g * PACK : (g + 1) * PACK, toks].rearrange("p t n -> p n t")
-            if engine == "vector":
-                nc.vector.tensor_copy(out=dst, in_=src)
-            else:
-                nc.scalar.copy(out=dst, in_=src)
+        def group_tokens(u, engine):
+            toks = slice(u * UNIT, (u + 1) * UNIT)
+            tile_ = grouped.tile([P, PASSES * UNIT * PACK], BF16, tag="h_grouped", align_bytes=64)
+            h_grouped[u] = tile_
+            for g in range(PASSES):
+                dst = tile_[:, g * UNIT * PACK : (g + 1) * UNIT * PACK].rearrange(
+                    "p (c i t) -> p c t i", i=4, t=PACK
+                )
+                src = h_planes[:, g * PACK : (g + 1) * PACK, toks].rearrange("p t (c i) -> p c t i", i=4)
+                if engine == "vector":
+                    nc.vector.tensor_copy(out=dst, in_=src)
+                else:
+                    nc.scalar.copy(out=dst, in_=src)
 
-        def pack_tokens(h, g):
-            toks = slice(h * HALF, (h + 1) * HALF)
+        def pack_tokens(u):
             nc.vector.quantize_mx(
-                out=h_words[:, g, toks].bitcast(FP8X4), scales=h_scales[:, g, toks],
-                in_=h_grouped[(h, g)][:],
+                out=h_words[:, u, :].bitcast(FP8X4), scales=h_scales[:, u, :], in_=h_grouped[u][:]
             )
 
-        def one_pass(acc, n, h, r, g, nt, start, stop):
-            toks = slice(h * HALF + r * P, h * HALF + (r + 1) * P)
+        def one_pass(acc, n, i, g, nt, start, stop):
+            u = i // UNIT_TILES
+            first = g * UNIT + (i % UNIT_TILES) * P
+            toks = slice(first, first + P)
             cols = slice(g * N_TILE, (g + 1) * N_TILE)
             nc.tensor.matmul_mx(
                 out=acc[:],
-                lhsT=h_words[:, g, toks].bitcast(FP8X4),
-                lhsT_scale=h_scales[:, g, toks],
+                lhsT=h_words[:, u, toks].bitcast(FP8X4),
+                lhsT_scale=h_scales[:, u, toks],
                 rhs=w_words[n][:, nt, cols].bitcast(FP8X4),
                 rhs_scale=w_scales[n][:, nt, cols],
                 start=start,
                 stop=stop,
             )
 
-        def queries(h, nt):
+        def queries(u, nt):
             cols = slice(nt * N_TILE, (nt + 1) * N_TILE)
-            for r in range(MERGE):
+            for a in range(UNIT_TILES):
+                i = u * UNIT_TILES + a
                 acc = banks.tile([P, N_TILE], F32, tag="bank")
                 for g in range(PASSES):
-                    one_pass(acc, "q", h, r, g, nt, g == 0, g == PASSES - 1)
+                    one_pass(acc, "q", i, g, nt, g == 0, g == PASSES - 1)
                 rows = results.tile([P, N_TILE], F32, tag="rows")
                 nc.vector.tensor_tensor(out=rows[:], in0=acc[:], in1=bias_all["q"][:, cols], op=ALU.add)
-                nc.sync.dma_start(out=q_view[:, h, r, cols], in_=rows[:])
+                nc.sync.dma_start(out=q_view[:, i // MERGE, i % MERGE, cols], in_=rows[:])
 
         def merged(n, h, nt):
             cols = slice(nt * N_TILE, (nt + 1) * N_TILE)
             acc = banks.tile([P, N_TILE], F32, tag="bank")
             for r in range(MERGE):
                 for g in range(PASSES):
-                    one_pass(acc, n, h, r, g, nt, r == 0 and g == 0, r == MERGE - 1 and g == PASSES - 1)
+                    one_pass(
+                        acc, n, h * MERGE + r, g, nt, r == 0 and g == 0, r == MERGE - 1 and g == PASSES - 1
+                    )
             rows = results.tile([P, N_TILE], F32, tag="rows")
             nc.vector.scalar_tensor_tensor(
                 out=rows[:], in0=acc[:], scalar=1.0 / MERGE, in1=bias_all[n][:, cols],
@@ -270,49 +293,60 @@ def tile_siglipencoderlayer_pa_kernel(
             )
             nc.sync.dma_start(out=merged_views[n][:, h, cols], in_=rows[:])
 
-        for i in range(RUN):
-            measure_tile(0, i)
-            flip_weight_bank("q", 0, i, "scalar")
-        finish_measure(0)
         flip_gain_bias()
-        for r in range(MERGE):
-            normalise(0, r, "gpsimd" if r % 2 == 0 else "scalar")
-        for r in range(MERGE):
-            measure_tile(1, r)
-        flip_tokens(0, 0, 0)
-        flip_tokens(0, 1, 0)
+        for n in "qkv":
+            spread_bias(n)
+        flip_weight_bank("q", 0, 0, "scalar")
+        measure(0)
+        flip_weight_bank("q", 0, 1, "scalar")
+        normalise(0, 0, "gpsimd")
+        normalise(0, 1, "scalar")
+        flip_weight_bank("q", 0, 2, "scalar")
+        flip_weight_bank("q", 0, 3, "scalar")
+        measure(1)
         pack_weight("q", 0)
-        group_tokens(0, 0, "vector")
-        pack_tokens(0, 0)
-        group_tokens(0, 1, "vector")
-        pack_tokens(0, 1)
-        finish_measure(1)
+        flip_tokens(0, 2)
+        group_tokens(0, "vector")
+        normalise(1, 0, "gpsimd")
+        normalise(1, 1, "scalar")
         flip_weight("q", 1, 0)
-        for r in range(MERGE):
-            normalise(1, r, "gpsimd" if r % 2 == 0 else "scalar")
+        pack_tokens(0)
+        flip_tokens(1, 2)
         queries(0, 0)
-        pack_weight("q", 1)
-        flip_tokens(1, 0, 0)
-        flip_tokens(1, 1, 0)
-        queries(0, 1)
-        group_tokens(1, 0, "vector")
-        pack_tokens(1, 0)
         flip_weight("k", 0, 0)
-        group_tokens(1, 1, "vector")
-        pack_tokens(1, 1)
+        pack_weight("q", 1)
         flip_weight("k", 1, 0)
+        group_tokens(1, "vector")
+        measure(2)
+        flip_weight("v", 0, 0)
+        normalise(2, 0, "gpsimd")
+        normalise(2, 1, "scalar")
+        pack_tokens(1)
+        queries(0, 1)
         queries(1, 0)
         pack_weight("k", 0)
         queries(1, 1)
+        flip_tokens(2, 0)
         pack_weight("k", 1)
-        flip_weight("v", 0, 0)
-        merged("k", 0, 0)
-        merged("k", 1, 0)
-        flip_weight("v", 1, 0)
         pack_weight("v", 0)
-        merged("k", 0, 1)
-        merged("k", 1, 1)
+        flip_weight("v", 1, 0)
+        measure(3)
+        group_tokens(2, "vector")
+        normalise(3, 0, "gpsimd")
+        normalise(3, 1, "scalar")
+        pack_tokens(2)
         pack_weight("v", 1)
-        for nt in range(N_TILES):
-            for h in range(HALVES):
-                merged("v", h, nt)
+        merged("k", 0, 0)
+        merged("k", 0, 1)
+        merged("v", 0, 0)
+        flip_tokens(3, 0)
+        group_tokens(3, "vector")
+        queries(2, 0)
+        pack_tokens(3)
+        merged("v", 0, 1)
+        queries(2, 1)
+        queries(3, 0)
+        queries(3, 1)
+        for n in "kv":
+            for nt in range(N_TILES):
+                merged(n, 1, nt)

from contextlib import ExitStack

import concourse.mybir as mybir
from concourse.masks import make_identity

F32 = mybir.dt.float32
BF16 = mybir.dt.bfloat16
U32 = mybir.dt.uint32
U8 = mybir.dt.uint8
FP8X4 = mybir.dt.float8_e4m3fn_x4
ACT = mybir.ActivationFunctionType
ALU = mybir.AluOpType

P = 128
TOKENS = 1024
D = 1024
E = 1024
MERGE = 4
EPS = 1e-6
PACK = 4
K_PASS = P * PACK
PASSES = D // K_PASS
CHUNKS = D // P
HALF = P * MERGE
HALVES = TOKENS // HALF
N_TILE = 512
N_TILES = E // N_TILE
RUN = N_TILE // P
BN_MAX = 512
TILES = TOKENS // P
UNIT_TILES = 2
UNITS = TILES // UNIT_TILES
UNIT = UNIT_TILES * P

FLOPS = 2 * 3 * TOKENS * D * E


def tile_siglipencoderlayer_pa_kernel(
    tc, x, ln1_g, ln1_b, Wq, bq, Wk, bk, Wv, bv, out_0, out_1, out_2
):
    nc = tc.nc
    x_view = x.flatten_outer_dims().rearrange("(h j r) d -> j h r d", h=HALVES, r=MERGE)
    q_view = out_0.flatten_outer_dims().rearrange("(h j r) e -> j h r e", h=HALVES, r=MERGE)
    merged_views = {
        "k": out_1.flatten_outer_dims().rearrange("(h j) e -> j h e", h=HALVES),
        "v": out_2.flatten_outer_dims().rearrange("(h j) e -> j h e", h=HALVES),
    }
    weights = {"q": Wq, "k": Wk, "v": Wv}
    biases = {"q": bq, "k": bk, "v": bv}

    with ExitStack() as stack:
        consts = stack.enter_context(tc.tile_pool(name="consts", bufs=1))
        raw = stack.enter_context(tc.tile_pool(name="raw", bufs=1))
        small = stack.enter_context(tc.tile_pool(name="small", bufs=2))
        normed = stack.enter_context(tc.tile_pool(name="normed", bufs=6))
        grouped = stack.enter_context(tc.tile_pool(name="grouped", bufs=3))
        packed = stack.enter_context(tc.tile_pool(name="packed", bufs=1))
        results = stack.enter_context(tc.tile_pool(name="results", bufs=8))
        banks = stack.enter_context(tc.psum_pool(name="banks", bufs=8))
        stack.enter_context(tc.manual_schedule())

        ident = consts.tile([P, P], F32, name="ident")
        make_identity(nc, ident[:])

        gb_rows = consts.tile([P, 2 * P], BF16, name="gb_rows")
        nc.vector.memset(gb_rows[:], 0.0)
        nc.scalar.dma_start(out=gb_rows[0:4, :], in_=ln1_g.rearrange("(c w) -> c w", c=4))
        nc.scalar.dma_start(out=gb_rows[4:8, :], in_=ln1_b.rearrange("(c w) -> c w", c=4))

        x_raw = [raw.tile([P, D], BF16, name="x_raw%d" % i) for i in range(TILES)]
        w_raw = {n: raw.tile([P, N_TILES, RUN * D], BF16, name="w_raw_" + n) for n in "qkv"}
        bias_rows = consts.tile([P, 3 * E], BF16, name="bias_rows")
        nc.vector.memset(bias_rows[:], 0.0)
        for k, n in enumerate("qkv"):
            nc.scalar.dma_start(
                out=bias_rows[0:1, k * E : (k + 1) * E], in_=biases[n].rearrange("(o e) -> o e", o=1)
            )
        ones = consts.tile([P, P], BF16, name="ones")
        nc.vector.memset(ones[:], 1.0)
        bias_all = {n: consts.tile([P, E], BF16, name="bias_all_" + n) for n in "qkv"}
        eps = consts.tile([P, 1], F32, name="eps")
        nc.vector.memset(eps[:], EPS)
        warm = consts.tile([P, 1], F32, name="warm")
        nc.scalar.activation(out=warm[:], in_=eps[:], func=ACT.Sqrt)

        def load_tokens(i):
            nc.sync.dma_start(out=x_raw[i][:], in_=x_view[:, i // MERGE, i % MERGE, :])

        def load_weight(n, nt, i):
            rows = weights[n].rearrange("(nt i p) d -> p nt i d", nt=N_TILES, p=P)
            nc.sync.dma_start(out=w_raw[n][:, nt, i * D : (i + 1) * D], in_=rows[:, nt, i, :])

        for i in range(TILES):
            load_tokens(i)
            load_weight("q", i // RUN, i % RUN)
        for n in "kv":
            for nt in range(N_TILES):
                for i in range(RUN):
                    load_weight(n, nt, i)

        gain_bias = consts.tile([P, 2 * CHUNKS], F32, name="gain_bias")
        h_planes = packed.tile([P, CHUNKS, TOKENS], BF16, name="h_planes")
        h_words = packed.tile([P, UNITS, PASSES * UNIT], U32, name="h_words", align_bytes=64)
        h_scales = packed.tile([P, UNITS, PASSES * UNIT], U8, name="h_scales", align_bytes=64)
        w_words = {
            n: packed.tile([P, N_TILES, PASSES * N_TILE], U32, name="w_words_" + n, align_bytes=64)
            for n in "qkv"
        }
        w_scales = {
            n: packed.tile([P, N_TILES, PASSES * N_TILE], U8, name="w_scales_" + n, align_bytes=64)
            for n in "qkv"
        }
        w_grouped = {}
        xn_tiles = {}
        moments = {}

        def spread_bias(n):
            first = "qkv".index(n) * E
            bank = banks.tile([P, E], BF16, tag="bank")
            for nt in range(N_TILES):
                cols = slice(nt * N_TILE, (nt + 1) * N_TILE)
                nc.tensor.matmul(
                    out=bank[:, cols],
                    lhsT=ones[:],
                    rhs=bias_rows[:, first + nt * N_TILE : first + (nt + 1) * N_TILE],
                    start=True,
                    stop=True,
                )
            nc.scalar.copy(out=bias_all[n][:], in_=bank[:])

        def flip_gain_bias():
            bank = banks.tile([P, N_TILE], F32, tag="bank")
            nc.tensor.transpose(out=bank[:, 0:P], in_=gb_rows[:].bitcast(F32), identity=ident[:])
            nc.vector.tensor_copy(out=gain_bias[:], in_=bank[:].bitcast(BF16)[:, 0 : 2 * CHUNKS])

        def flip_weight_bank(n, nt, i, engine):
            if i == 0:
                w_grouped[(n, nt)] = grouped.tile(
                    [P, PASSES * N_TILE * PACK], BF16, name="w_grouped", tag="w_grouped", align_bytes=64
                )
            words_in = w_raw[n][:, nt, :].bitcast(F32).rearrange(
                "p (i c q) -> p i c q", i=RUN, c=PASSES * 2
            )
            words_out = w_grouped[(n, nt)][:].bitcast(F32).rearrange(
                "p (g e u) -> p g e u", g=PASSES, u=2
            )
            bank = banks.tile([P, N_TILE], F32, tag="bank")
            for c in range(PASSES * 2):
                nc.tensor.transpose(
                    out=bank[:, c * P : (c + 1) * P], in_=words_in[:, i, c, :], identity=ident[:]
                )
            dst = words_out[:, :, i * P : (i + 1) * P, :]
            src = bank[:].rearrange("p (g u e) -> p g e u", g=PASSES, u=2)
            if engine == "vector":
                nc.vector.tensor_copy(out=dst, in_=src)
            else:
                nc.scalar.copy(out=dst, in_=src)

        def flip_weight(n, nt, vector_banks):
            for i in range(RUN):
                flip_weight_bank(n, nt, i, "vector" if i < vector_banks else "scalar")

        def pack_weight(n, nt):
            nc.vector.quantize_mx(
                out=w_words[n][:, nt, :].bitcast(FP8X4),
                scales=w_scales[n][:, nt, :],
                in_=w_grouped[(n, nt)][:],
            )

        def measure(u):
            mean_var = small.tile([P, UNIT_TILES, 2], F32, tag="mean_var")
            for a in range(UNIT_TILES):
                stats = small.tile([P, D // BN_MAX, 6], F32, tag="stats")
                for s in range(D // BN_MAX):
                    nc.vector.bn_stats(
                        out=stats[:, s, :], in_=x_raw[u * UNIT_TILES + a][:, s * BN_MAX : (s + 1) * BN_MAX]
                    )
                nc.vector.bn_aggr(out=mean_var[:, a, :], in_=stats[:].rearrange("p s k -> p (s k)"))
            std = small.tile([P, UNIT_TILES], F32, tag="std")
            nc.scalar.activation(out=std[:], in_=mean_var[:, :, 1], func=ACT.Sqrt, bias=eps[:, 0:1])
            rstd = small.tile([P, UNIT_TILES], F32, tag="rstd")
            nc.vector.reciprocal(out=rstd[:], in_=std[:])
            shift = small.tile([P, UNIT_TILES], F32, tag="shift")
            nc.vector.scalar_tensor_tensor(
                out=shift[:], in0=mean_var[:, :, 0], scalar=-1.0, in1=rstd[:], op0=ALU.mult, op1=ALU.mult
            )
            moments[u] = (rstd, shift)

        def normalise(u, a, engine):
            rstd, shift = moments[u]
            xn = normed.tile([P, D], F32, tag="xn")
            xn_tiles[(u, a)] = xn
            dst = xn[:].rearrange("p (c e q) -> p c e q", c=PASSES * 2, e=2)
            src = x_raw[u * UNIT_TILES + a][:].rearrange("p (c q e) -> p c e q", c=PASSES * 2, e=2)
            if engine == "scalar":
                nc.scalar.activation(
                    out=dst, in_=src, func=ACT.Identity, scale=rstd[:, a : a + 1], bias=shift[:, a : a + 1]
                )
            else:
                nc.gpsimd.tensor_scalar(
                    out=dst, in0=src, scalar1=rstd[:, a : a + 1], scalar2=shift[:, a : a + 1],
                    op0=ALU.mult, op1=ALU.add,
                )

        def flip_tokens(u, vector_banks):
            toks = slice(u * UNIT, (u + 1) * UNIT)
            per_bank = RUN // UNIT_TILES
            for b in range(CHUNKS // per_bank):
                bank = banks.tile([P, N_TILE], F32, tag="bank")
                for k in range(per_bank):
                    f = b * per_bank + k
                    for a in range(UNIT_TILES):
                        col = (k * UNIT_TILES + a) * P
                        nc.tensor.transpose(
                            out=bank[:, col : col + P],
                            in_=xn_tiles[(u, a)][:, f * P : (f + 1) * P],
                            identity=ident[:],
                        )
                for k in range(per_bank):
                    f = b * per_bank + k
                    gain = gain_bias[:, f : f + 1]
                    bias = gain_bias[:, CHUNKS + f : CHUNKS + f + 1]
                    src = bank[:, k * UNIT : (k + 1) * UNIT]
                    if b < vector_banks:
                        nc.vector.tensor_scalar(
                            out=h_planes[:, f, toks], in0=src, scalar1=gain, scalar2=bias,
                            op0=ALU.mult, op1=ALU.add,
                        )
                    else:
                        nc.scalar.activation(
                            out=h_planes[:, f, toks], in_=src, func=ACT.Identity, scale=gain, bias=bias
                        )

        h_grouped = {}

        def group_tokens(u, engine):
            toks = slice(u * UNIT, (u + 1) * UNIT)
            tile_ = grouped.tile([P, PASSES * UNIT * PACK], BF16, tag="h_grouped", align_bytes=64)
            h_grouped[u] = tile_
            for g in range(PASSES):
                dst = tile_[:, g * UNIT * PACK : (g + 1) * UNIT * PACK].rearrange(
                    "p (c i t) -> p c t i", i=4, t=PACK
                )
                src = h_planes[:, g * PACK : (g + 1) * PACK, toks].rearrange("p t (c i) -> p c t i", i=4)
                if engine == "vector":
                    nc.vector.tensor_copy(out=dst, in_=src)
                else:
                    nc.scalar.copy(out=dst, in_=src)

        def pack_tokens(u):
            nc.vector.quantize_mx(
                out=h_words[:, u, :].bitcast(FP8X4), scales=h_scales[:, u, :], in_=h_grouped[u][:]
            )

        def one_pass(acc, n, i, g, nt, start, stop):
            u = i // UNIT_TILES
            first = g * UNIT + (i % UNIT_TILES) * P
            toks = slice(first, first + P)
            cols = slice(g * N_TILE, (g + 1) * N_TILE)
            nc.tensor.matmul_mx(
                out=acc[:],
                lhsT=h_words[:, u, toks].bitcast(FP8X4),
                lhsT_scale=h_scales[:, u, toks],
                rhs=w_words[n][:, nt, cols].bitcast(FP8X4),
                rhs_scale=w_scales[n][:, nt, cols],
                start=start,
                stop=stop,
            )

        def queries(u, nt):
            cols = slice(nt * N_TILE, (nt + 1) * N_TILE)
            for a in range(UNIT_TILES):
                i = u * UNIT_TILES + a
                acc = banks.tile([P, N_TILE], F32, tag="bank")
                for g in range(PASSES):
                    one_pass(acc, "q", i, g, nt, g == 0, g == PASSES - 1)
                rows = results.tile([P, N_TILE], F32, tag="rows")
                nc.vector.tensor_tensor(out=rows[:], in0=acc[:], in1=bias_all["q"][:, cols], op=ALU.add)
                nc.sync.dma_start(out=q_view[:, i // MERGE, i % MERGE, cols], in_=rows[:])

        def merged(n, h, nt):
            cols = slice(nt * N_TILE, (nt + 1) * N_TILE)
            acc = banks.tile([P, N_TILE], F32, tag="bank")
            for r in range(MERGE):
                for g in range(PASSES):
                    one_pass(
                        acc, n, h * MERGE + r, g, nt, r == 0 and g == 0, r == MERGE - 1 and g == PASSES - 1
                    )
            rows = results.tile([P, N_TILE], F32, tag="rows")
            nc.vector.scalar_tensor_tensor(
                out=rows[:], in0=acc[:], scalar=1.0 / MERGE, in1=bias_all[n][:, cols],
                op0=ALU.mult, op1=ALU.add,
            )
            nc.sync.dma_start(out=merged_views[n][:, h, cols], in_=rows[:])

        flip_gain_bias()
        for n in "qkv":
            spread_bias(n)
        flip_weight_bank("q", 0, 0, "scalar")
        measure(0)
        flip_weight_bank("q", 0, 1, "scalar")
        normalise(0, 0, "gpsimd")
        normalise(0, 1, "scalar")
        flip_weight_bank("q", 0, 2, "scalar")
        flip_weight_bank("q", 0, 3, "scalar")
        measure(1)
        pack_weight("q", 0)
        flip_tokens(0, 2)
        group_tokens(0, "vector")
        normalise(1, 0, "gpsimd")
        normalise(1, 1, "scalar")
        flip_weight("q", 1, 0)
        pack_tokens(0)
        flip_tokens(1, 2)
        queries(0, 0)
        flip_weight("k", 0, 0)
        pack_weight("q", 1)
        flip_weight("k", 1, 0)
        group_tokens(1, "vector")
        measure(2)
        flip_weight("v", 0, 0)
        normalise(2, 0, "gpsimd")
        normalise(2, 1, "scalar")
        pack_tokens(1)
        queries(0, 1)
        queries(1, 0)
        pack_weight("k", 0)
        queries(1, 1)
        flip_tokens(2, 0)
        pack_weight("k", 1)
        pack_weight("v", 0)
        flip_weight("v", 1, 0)
        measure(3)
        group_tokens(2, "vector")
        normalise(3, 0, "gpsimd")
        normalise(3, 1, "scalar")
        pack_tokens(2)
        pack_weight("v", 1)
        merged("k", 0, 0)
        merged("k", 0, 1)
        merged("v", 0, 0)
        flip_tokens(3, 0)
        group_tokens(3, "vector")
        queries(2, 0)
        pack_tokens(3)
        merged("v", 0, 1)
        queries(2, 1)
        queries(3, 0)
        queries(3, 1)
        for n in "kv":
            for nt in range(N_TILES):
                merged(n, 1, nt)
